import numpy as np
import ml_dtypes


def mxq(x, axis, fmt="e4m3"):
    dtype, down = {"e4m3": (ml_dtypes.float8_e4m3fn, 7), "e5m2": (ml_dtypes.float8_e5m2, 14)}[fmt]
    v = np.moveaxis(np.asarray(x, np.float32).astype(ml_dtypes.bfloat16).astype(np.float64), axis, -1)
    blocks = v.reshape(v.shape[:-1] + (-1, 32))
    amax = np.abs(blocks).max(-1, keepdims=True)
    byte = np.maximum(np.where(amax > 0, np.frexp(amax)[1] - 1 + 127, 0) - down, 1)
    scale = np.exp2(byte - 127.0)
    codes = (blocks / scale).astype(np.float32).astype(dtype).astype(np.float64)
    return np.moveaxis((codes * scale).reshape(v.shape), -1, axis)


WIDE = False


def mx_kscale(k):
    if not WIDE:
        return np.ones(k)
    levels = np.array([10, -10, 5, -5, 0])
    a = np.random.permutation(np.resize(levels, k // 512 * 4)).reshape(k // 512, 4)
    idx = np.arange(k)
    return np.exp2(a[idx // 512, idx % 128 // 32])


BF16 = ml_dtypes.bfloat16


def bf(x):
    return np.asarray(x, np.float32).astype(BF16)


def f64(x):
    return np.asarray(x).astype(np.float64)


B, R, C, H, DH = 64, 8, 1024, 4, 128
T = R * R
E = H * DH
EPS = 2.0 ** -23


def rmsnorm(v):
    return v * (1.0 / np.sqrt(np.mean(np.square(v), axis=-1, keepdims=True) + EPS))


def setup_inputs():
    s = mx_kscale(C)
    return {"x": bf(np.random.standard_normal((B, T, C)) * s),
            "Wq": bf(np.random.standard_normal((C, E)) / np.sqrt(C) / s[:, None]),
            "Wk": bf(np.random.standard_normal((C, E)) / np.sqrt(C) / s[:, None])}


def reference(x, Wq, Wk):
    xq = mxq(f64(x), 2, "e4m3")

    def proj(W):
        return (xq @ mxq(f64(W), 0, "e4m3")).reshape(B, T, H, DH).transpose(0, 2, 1, 3)

    return rmsnorm(proj(Wq)), rmsnorm(proj(Wk))

@@ -1,0 +1,204 @@
+from contextlib import ExitStack
+
+import concourse.mybir as mybir
+from concourse.masks import make_identity
+
+F32 = mybir.dt.float32
+BF16 = mybir.dt.bfloat16
+U32 = mybir.dt.uint32
+U8 = mybir.dt.uint8
+FP8X4 = mybir.dt.float8_e4m3fn_x4
+ACT = mybir.ActivationFunctionType
+ALU = mybir.AluOpType
+
+P = 128
+BOARDS, SQUARES, C = 64, 64, 1024
+H, DH = 4, 128
+E = H * DH
+EPS = 2.0**-23
+TOKENS = BOARDS * SQUARES
+
+PACK = 4
+K_PASS = P * PACK
+PASSES = C // K_PASS
+WORD_PLANES = 2
+
+GROUP_TILES = 8
+GROUP_TOKENS = P * GROUP_TILES
+GROUP_BOARDS = GROUP_TOKENS // SQUARES
+RUNS = SQUARES // GROUP_TILES
+BLOCK_TILES = 4
+PAIR = 2
+BLOCKS = TOKENS // (P * BLOCK_TILES)
+BLOCKS_IN_GROUP = GROUP_TILES // BLOCK_TILES
+PAIRS_IN_BLOCK = BLOCK_TILES // PAIR
+
+FLOPS = 2 * TOKENS * C * 2 * E
+
+
+def load_weight(nc, pool, w):
+    w_raw = pool.tile([P, PASSES, PACK, E], BF16)
+    for g in range(PASSES):
+        nc.sync.dma_start(
+            out=w_raw[:, g, :, :].rearrange("p (u e) n -> p u (e n)", u=WORD_PLANES),
+            in_=w[g * K_PASS : (g + 1) * K_PASS, :].rearrange(
+                "(u p e) n -> p u (e n)", u=WORD_PLANES, p=P
+            ),
+        )
+    return w_raw
+
+
+def quantise_weight(nc, pool, w_raw, w_codes, w_scales, half):
+    for g in range(PASSES):
+        w_grouped = pool.tile([P, E, PACK], BF16, align_bytes=64)
+        nc.vector.tensor_copy(
+            out=w_grouped[:].rearrange("p (c i) t -> p c t i", i=4),
+            in_=w_raw[:, g, :, :].rearrange("p t (c i) -> p c t i", i=4),
+        )
+        nc.vector.quantize_mx(
+            out=w_codes[:, g, half, :].bitcast(FP8X4),
+            scales=w_scales[:, g, half, :],
+            in_=w_grouped[:].rearrange("p n t -> p (n t)"),
+        )
+
+
+def load_tokens(nc, pool, x_tiles, blk):
+    grp, first = divmod(blk * BLOCK_TILES, GROUP_TILES)
+    x_sb = pool.tile([P, BLOCK_TILES, C], BF16)
+    for pair in range(PAIRS_IN_BLOCK):
+        nc.sync.dma_start(
+            out=x_sb[:, pair * PAIR : (pair + 1) * PAIR, :],
+            in_=x_tiles[grp, :, first + pair * PAIR : first + (pair + 1) * PAIR, :],
+        )
+    return x_sb
+
+
+def quantise_tokens(nc, pools, ident, x_sb, pair):
+    x_grouped = pools["stage"].tile([P, PAIR, PASSES, P, PACK], BF16, align_bytes=64)
+    for j in range(PAIR):
+        words = x_sb[:, pair * PAIR + j, :].bitcast(F32)
+        turned = pools["psum_x"].tile([P, PASSES * WORD_PLANES, P], F32)
+        for c in range(PASSES * WORD_PLANES):
+            nc.tensor.transpose(turned[:, c, :], words[:, c * P : (c + 1) * P], ident[:])
+        copy = nc.scalar.copy if j == 0 else nc.vector.tensor_copy
+        copy(
+            out=x_grouped[:, j]
+            .rearrange("p g r t -> p (g r t)")
+            .bitcast(F32)
+            .rearrange("p (g r u) -> p g r u", g=PASSES, u=WORD_PLANES),
+            in_=turned[:].rearrange("p (g u) r -> p g r u", u=WORD_PLANES),
+        )
+    x_codes = pools["codes"].tile([P, PAIR, PASSES, P], U32, align_bytes=64)
+    x_scales = pools["codes"].tile([P, PAIR, PASSES, P], U8, align_bytes=64)
+    nc.vector.quantize_mx(
+        out=x_codes[:].rearrange("p j g r -> p (j g r)").bitcast(FP8X4),
+        scales=x_scales[:].rearrange("p j g r -> p (j g r)"),
+        in_=x_grouped[:].rearrange("p j g r t -> p (j g r t)"),
+    )
+    return x_codes, x_scales
+
+
+def tile_pieceroutedattention_pa_t_kernel(tc, x, Wq, Wk, out_0, out_1):
+    nc = tc.nc
+    x_tiles = x.flatten_outer_dims().rearrange("(g p i) c -> g p i c", p=P, i=GROUP_TILES)
+    out_runs = [
+        out.rearrange("b h (r i) d -> h b r (i d)", i=GROUP_TILES) for out in (out_0, out_1)
+    ]
+
+    with ExitStack() as stack:
+        keep = stack.enter_context(tc.tile_pool(name="keep", bufs=1))
+        w_pool = stack.enter_context(tc.tile_pool(name="w", bufs=2))
+        x_pool = stack.enter_context(tc.tile_pool(name="x", bufs=BLOCKS))
+        pools = {
+            "stage": stack.enter_context(tc.tile_pool(name="stage", bufs=3)),
+            "codes": stack.enter_context(tc.tile_pool(name="codes", bufs=2 * PAIRS_IN_BLOCK + 1)),
+            "psum_x": stack.enter_context(tc.psum_pool(name="psum_x", bufs=2)),
+        }
+        psum_y = stack.enter_context(tc.psum_pool(name="psum_y", bufs=6))
+        small = stack.enter_context(tc.tile_pool(name="small", bufs=4))
+        res_pool = stack.enter_context(tc.tile_pool(name="res", bufs=4))
+
+        w_raw = [load_weight(nc, w_pool, Wq)]
+        x_blocks = [load_tokens(nc, x_pool, x_tiles, 0)]
+        w_raw.append(load_weight(nc, w_pool, Wk))
+        for blk in range(1, BLOCKS):
+            x_blocks.append(load_tokens(nc, x_pool, x_tiles, blk))
+
+        ident = keep.tile([P, P], F32)
+        make_identity(nc, ident[:])
+        eps = keep.tile([P, 1], F32)
+        nc.vector.memset(eps[:], EPS)
+        warm = keep.tile([P, 1], F32)
+        nc.scalar.activation(out=warm[:], in_=eps[:], func=ACT.Abs_reciprocal_sqrt)
+
+        w_codes = keep.tile([P, PASSES, 2, E], U32, align_bytes=64)
+        w_scales = keep.tile([P, PASSES, 2, E], U8, align_bytes=64)
+
+        quantise_weight(nc, w_pool, w_raw[0], w_codes, w_scales, 0)
+        quantised = [
+            quantise_tokens(nc, pools, ident, x_blocks[0], pair) for pair in range(PAIRS_IN_BLOCK)
+        ]
+        quantise_weight(nc, w_pool, w_raw[1], w_codes, w_scales, 1)
+
+        for blk in range(BLOCKS):
+            grp, part = divmod(blk, BLOCKS_IN_GROUP)
+            current = quantised
+            if blk + 1 < BLOCKS:
+                quantised = [
+                    quantise_tokens(nc, pools, ident, x_blocks[blk + 1], pair)
+                    for pair in range(PAIRS_IN_BLOCK)
+                ]
+            for half in range(2):
+                res = res_pool.tile([P, H, BLOCK_TILES, DH], F32)
+                for pair in range(PAIRS_IN_BLOCK):
+                    x_codes, x_scales = current[pair]
+                    sums = []
+                    for j in range(PAIR):
+                        y = psum_y.tile([P, E], F32)
+                        for g in range(PASSES):
+                            nc.tensor.matmul_mx(
+                                out=y[:],
+                                lhsT=x_codes[:, j, g, :].bitcast(FP8X4),
+                                lhsT_scale=x_scales[:, j, g, :],
+                                rhs=w_codes[:, g, half, :].bitcast(FP8X4),
+                                rhs_scale=w_scales[:, g, half, :],
+                                start=(g == 0),
+                                stop=(g == PASSES - 1),
+                            )
+                        sums.append(y)
+                    squares = small.tile([P, PAIR, H, DH], BF16)
+                    sum_sq = small.tile([P, PAIR, H], F32)
+                    for j in range(PAIR):
+                        for h in range(H):
+                            nc.scalar.activation(
+                                out=squares[:, j, h, :],
+                                in_=sums[j][:, h * DH : (h + 1) * DH],
+                                func=ACT.Square,
+                                accum_out=sum_sq[:, j, h : h + 1],
+                            )
+                    inv_rms = small.tile([P, PAIR, H], F32)
+                    nc.scalar.activation(
+                        out=inv_rms[:],
+                        in_=sum_sq[:],
+                        func=ACT.Abs_reciprocal_sqrt,
+                        scale=1.0 / DH,
+                        bias=eps[:, 0:1],
+                    )
+                    for j in range(PAIR):
+                        nc.vector.tensor_tensor(
+                            out=res[:, :, pair * PAIR + j, :],
+                            in0=sums[j][:].rearrange("p (h d) -> p h d", h=H),
+                            in1=inv_rms[:, j, :].unsqueeze(2).to_broadcast([P, H, DH]),
+                            op=ALU.mult,
+                        )
+                run = BLOCK_TILES * DH
+                for h in range(H):
+                    nc.sync.dma_start(
+                        out=out_runs[half][
+                            h,
+                            grp * GROUP_BOARDS : (grp + 1) * GROUP_BOARDS,
+                            :,
+                            part * run : (part + 1) * run,
+                        ],
+                        in_=res[:, h, :, :].rearrange("p i d -> p (i d)"),
+                    )

@@ -32,165 +32,175 @@ PAIR = 2
 BLOCKS = TOKENS // (P * BLOCK_TILES)
 BLOCKS_IN_GROUP = GROUP_TILES // BLOCK_TILES
 PAIRS_IN_BLOCK = BLOCK_TILES // PAIR
+PAIRS = BLOCKS * PAIRS_IN_BLOCK
+UNITS_IN_BLOCK = 2 * PAIRS_IN_BLOCK
+UNITS = BLOCKS * UNITS_IN_BLOCK
+PAIRS_AHEAD = 2
 
 FLOPS = 2 * TOKENS * C * 2 * E
 
 
-def load_weight(nc, pool, w):
-    w_raw = pool.tile([P, PASSES, PACK, E], BF16)
-    for g in range(PASSES):
-        nc.sync.dma_start(
-            out=w_raw[:, g, :, :].rearrange("p (u e) n -> p u (e n)", u=WORD_PLANES),
-            in_=w[g * K_PASS : (g + 1) * K_PASS, :].rearrange(
-                "(u p e) n -> p u (e n)", u=WORD_PLANES, p=P
-            ),
-        )
-    return w_raw
-
-
-def quantise_weight(nc, pool, w_raw, w_codes, w_scales, half):
-    for g in range(PASSES):
-        w_grouped = pool.tile([P, E, PACK], BF16, align_bytes=64)
-        nc.vector.tensor_copy(
-            out=w_grouped[:].rearrange("p (c i) t -> p c t i", i=4),
-            in_=w_raw[:, g, :, :].rearrange("p t (c i) -> p c t i", i=4),
-        )
-        nc.vector.quantize_mx(
-            out=w_codes[:, g, half, :].bitcast(FP8X4),
-            scales=w_scales[:, g, half, :],
-            in_=w_grouped[:].rearrange("p n t -> p (n t)"),
-        )
-
-
-def load_tokens(nc, pool, x_tiles, blk):
-    grp, first = divmod(blk * BLOCK_TILES, GROUP_TILES)
-    x_sb = pool.tile([P, BLOCK_TILES, C], BF16)
-    for pair in range(PAIRS_IN_BLOCK):
-        nc.sync.dma_start(
-            out=x_sb[:, pair * PAIR : (pair + 1) * PAIR, :],
-            in_=x_tiles[grp, :, first + pair * PAIR : first + (pair + 1) * PAIR, :],
-        )
-    return x_sb
-
-
-def quantise_tokens(nc, pools, ident, x_sb, pair):
-    x_grouped = pools["stage"].tile([P, PAIR, PASSES, P, PACK], BF16, align_bytes=64)
-    for j in range(PAIR):
-        words = x_sb[:, pair * PAIR + j, :].bitcast(F32)
-        turned = pools["psum_x"].tile([P, PASSES * WORD_PLANES, P], F32)
-        for c in range(PASSES * WORD_PLANES):
-            nc.tensor.transpose(turned[:, c, :], words[:, c * P : (c + 1) * P], ident[:])
-        copy = nc.scalar.copy if j == 0 else nc.vector.tensor_copy
-        copy(
-            out=x_grouped[:, j]
-            .rearrange("p g r t -> p (g r t)")
-            .bitcast(F32)
-            .rearrange("p (g r u) -> p g r u", g=PASSES, u=WORD_PLANES),
-            in_=turned[:].rearrange("p (g u) r -> p g r u", u=WORD_PLANES),
-        )
-    x_codes = pools["codes"].tile([P, PAIR, PASSES, P], U32, align_bytes=64)
-    x_scales = pools["codes"].tile([P, PAIR, PASSES, P], U8, align_bytes=64)
-    nc.vector.quantize_mx(
-        out=x_codes[:].rearrange("p j g r -> p (j g r)").bitcast(FP8X4),
-        scales=x_scales[:].rearrange("p j g r -> p (j g r)"),
-        in_=x_grouped[:].rearrange("p j g r t -> p (j g r t)"),
-    )
-    return x_codes, x_scales
-
-
 def tile_pieceroutedattention_pa_t_kernel(tc, x, Wq, Wk, out_0, out_1):
     nc = tc.nc
+    weights = (Wq, Wk)
     x_tiles = x.flatten_outer_dims().rearrange("(g p i) c -> g p i c", p=P, i=GROUP_TILES)
     out_runs = [
         out.rearrange("b h (r i) d -> h b r (i d)", i=GROUP_TILES) for out in (out_0, out_1)
     ]
 
     with ExitStack() as stack:
+        stack.enter_context(tc.manual_schedule())
         keep = stack.enter_context(tc.tile_pool(name="keep", bufs=1))
         w_pool = stack.enter_context(tc.tile_pool(name="w", bufs=2))
         x_pool = stack.enter_context(tc.tile_pool(name="x", bufs=BLOCKS))
-        pools = {
-            "stage": stack.enter_context(tc.tile_pool(name="stage", bufs=3)),
-            "codes": stack.enter_context(tc.tile_pool(name="codes", bufs=2 * PAIRS_IN_BLOCK + 1)),
-            "psum_x": stack.enter_context(tc.psum_pool(name="psum_x", bufs=2)),
-        }
-        psum_y = stack.enter_context(tc.psum_pool(name="psum_y", bufs=6))
+        stage = stack.enter_context(tc.tile_pool(name="stage", bufs=2))
+        codes_pool = stack.enter_context(tc.tile_pool(name="codes", bufs=2 * PAIRS_IN_BLOCK + 1))
         small = stack.enter_context(tc.tile_pool(name="small", bufs=4))
-        res_pool = stack.enter_context(tc.tile_pool(name="res", bufs=4))
+        res_pool = stack.enter_context(tc.tile_pool(name="res", bufs=6))
+        psum_x = stack.enter_context(tc.psum_pool(name="psum_x", bufs=PAIR))
+        psum_y = stack.enter_context(tc.psum_pool(name="psum_y", bufs=3 * PAIR))
 
-        w_raw = [load_weight(nc, w_pool, Wq)]
-        x_blocks = [load_tokens(nc, x_pool, x_tiles, 0)]
-        w_raw.append(load_weight(nc, w_pool, Wk))
-        for blk in range(1, BLOCKS):
-            x_blocks.append(load_tokens(nc, x_pool, x_tiles, blk))
+        w_raw = {}
+        w_grouped = {}
+        x_blocks = {}
+        turned = {}
+        grouped = {}
+        quantised = {}
+        sums = {}
+        sum_sq = {}
+        inv_rms = {}
+        results = {}
 
-        ident = keep.tile([P, P], F32)
-        make_identity(nc, ident[:])
-        eps = keep.tile([P, 1], F32)
-        nc.vector.memset(eps[:], EPS)
-        warm = keep.tile([P, 1], F32)
-        nc.scalar.activation(out=warm[:], in_=eps[:], func=ACT.Abs_reciprocal_sqrt)
+        def load_weight(half):
+            raw = w_pool.tile([P, PASSES, PACK, E], BF16)
+            for g in range(PASSES):
+                nc.sync.dma_start(
+                    out=raw[:, g, :, :].rearrange("p (u e) n -> p u (e n)", u=WORD_PLANES),
+                    in_=weights[half][g * K_PASS : (g + 1) * K_PASS, :].rearrange(
+                        "(u p e) n -> p u (e n)", u=WORD_PLANES, p=P
+                    ),
+                )
+            w_raw[half] = raw
 
-        w_codes = keep.tile([P, PASSES, 2, E], U32, align_bytes=64)
-        w_scales = keep.tile([P, PASSES, 2, E], U8, align_bytes=64)
+        def load_tokens(blk):
+            grp, first = divmod(blk * BLOCK_TILES, GROUP_TILES)
+            x_sb = x_pool.tile([P, BLOCK_TILES, C], BF16)
+            for pr in range(PAIRS_IN_BLOCK):
+                nc.sync.dma_start(
+                    out=x_sb[:, pr * PAIR : (pr + 1) * PAIR, :],
+                    in_=x_tiles[grp, :, first + pr * PAIR : first + (pr + 1) * PAIR, :],
+                )
+            x_blocks[blk] = x_sb
 
-        quantise_weight(nc, w_pool, w_raw[0], w_codes, w_scales, 0)
-        quantised = [
-            quantise_tokens(nc, pools, ident, x_blocks[0], pair) for pair in range(PAIRS_IN_BLOCK)
-        ]
-        quantise_weight(nc, w_pool, w_raw[1], w_codes, w_scales, 1)
+        def regroup_weight(half, g):
+            side_by_side = w_pool.tile([P, E, PACK], BF16, align_bytes=64)
+            nc.vector.tensor_copy(
+                out=side_by_side[:].rearrange("p (c i) t -> p c t i", i=4),
+                in_=w_raw[half][:, g, :, :].rearrange("p t (c i) -> p c t i", i=4),
+            )
+            w_grouped[(half, g)] = side_by_side
 
-        for blk in range(BLOCKS):
-            grp, part = divmod(blk, BLOCKS_IN_GROUP)
-            current = quantised
-            if blk + 1 < BLOCKS:
-                quantised = [
-                    quantise_tokens(nc, pools, ident, x_blocks[blk + 1], pair)
-                    for pair in range(PAIRS_IN_BLOCK)
-                ]
-            for half in range(2):
-                res = res_pool.tile([P, H, BLOCK_TILES, DH], F32)
-                for pair in range(PAIRS_IN_BLOCK):
-                    x_codes, x_scales = current[pair]
-                    sums = []
-                    for j in range(PAIR):
-                        y = psum_y.tile([P, E], F32)
-                        for g in range(PASSES):
-                            nc.tensor.matmul_mx(
-                                out=y[:],
-                                lhsT=x_codes[:, j, g, :].bitcast(FP8X4),
-                                lhsT_scale=x_scales[:, j, g, :],
-                                rhs=w_codes[:, g, half, :].bitcast(FP8X4),
-                                rhs_scale=w_scales[:, g, half, :],
-                                start=(g == 0),
-                                stop=(g == PASSES - 1),
-                            )
-                        sums.append(y)
-                    squares = small.tile([P, PAIR, H, DH], BF16)
-                    sum_sq = small.tile([P, PAIR, H], F32)
-                    for j in range(PAIR):
-                        for h in range(H):
-                            nc.scalar.activation(
-                                out=squares[:, j, h, :],
-                                in_=sums[j][:, h * DH : (h + 1) * DH],
-                                func=ACT.Square,
-                                accum_out=sum_sq[:, j, h : h + 1],
-                            )
-                    inv_rms = small.tile([P, PAIR, H], F32)
-                    nc.scalar.activation(
-                        out=inv_rms[:],
-                        in_=sum_sq[:],
-                        func=ACT.Abs_reciprocal_sqrt,
-                        scale=1.0 / DH,
-                        bias=eps[:, 0:1],
+        def quantise_weight(half, g):
+            nc.vector.quantize_mx(
+                out=w_codes[:, g, half, :].bitcast(FP8X4),
+                scales=w_scales[:, g, half, :],
+                in_=w_grouped[(half, g)][:].rearrange("p n t -> p (n t)"),
+            )
+
+        def turn(pair):
+            blk, pr = divmod(pair, PAIRS_IN_BLOCK)
+            banks = []
+            for j in range(PAIR):
+                words = x_blocks[blk][:, pr * PAIR + j, :].bitcast(F32)
+                bank = psum_x.tile([P, PASSES * WORD_PLANES, P], F32)
+                for c in range(PASSES * WORD_PLANES):
+                    nc.tensor.transpose(bank[:, c, :], words[:, c * P : (c + 1) * P], ident[:])
+                banks.append(bank)
+            turned[pair] = banks
+            side_by_side = stage.tile([P, PAIR, PASSES, P, PACK], BF16, align_bytes=64)
+            grouped[pair] = side_by_side
+
+        def regroup_tokens(pair, j, copy):
+            copy(
+                out=grouped[pair][:, j]
+                .rearrange("p g r t -> p (g r t)")
+                .bitcast(F32)
+                .rearrange("p (g r u) -> p g r u", g=PASSES, u=WORD_PLANES),
+                in_=turned[pair][j][:].rearrange("p (g u) r -> p g r u", u=WORD_PLANES),
+            )
+
+        def quantise_tokens(pair):
+            x_codes = codes_pool.tile([P, PAIR, PASSES, P], U32, align_bytes=64)
+            x_scales = codes_pool.tile([P, PAIR, PASSES, P], U8, align_bytes=64)
+            nc.vector.quantize_mx(
+                out=x_codes[:].rearrange("p j g r -> p (j g r)").bitcast(FP8X4),
+                scales=x_scales[:].rearrange("p j g r -> p (j g r)"),
+                in_=grouped[pair][:].rearrange("p j g r t -> p (j g r t)"),
+            )
+            quantised[pair] = (x_codes, x_scales)
+
+        def place(unit):
+            blk, rest = divmod(unit, UNITS_IN_BLOCK)
+            half, pr = divmod(rest, PAIRS_IN_BLOCK)
+            return blk, half, pr
+
+        def project(unit):
+            blk, half, pr = place(unit)
+            x_codes, x_scales = quantised[blk * PAIRS_IN_BLOCK + pr]
+            banks = []
+            for j in range(PAIR):
+                y = psum_y.tile([P, E], F32)
+                for g in range(PASSES):
+                    nc.tensor.matmul_mx(
+                        out=y[:],
+                        lhsT=x_codes[:, j, g, :].bitcast(FP8X4),
+                        lhsT_scale=x_scales[:, j, g, :],
+                        rhs=w_codes[:, g, half, :].bitcast(FP8X4),
+                        rhs_scale=w_scales[:, g, half, :],
+                        start=(g == 0),
+                        stop=(g == PASSES - 1),
                     )
-                    for j in range(PAIR):
-                        nc.vector.tensor_tensor(
-                            out=res[:, :, pair * PAIR + j, :],
-                            in0=sums[j][:].rearrange("p (h d) -> p h d", h=H),
-                            in1=inv_rms[:, j, :].unsqueeze(2).to_broadcast([P, H, DH]),
-                            op=ALU.mult,
-                        )
+                banks.append(y)
+            sums[unit] = banks
+            totals = small.tile([P, PAIR, H], F32)
+            sum_sq[unit] = totals
+
+        def sum_squares(unit, j):
+            squares = small.tile([P, H, DH], BF16)
+            for h in range(H):
+                nc.scalar.activation(
+                    out=squares[:, h, :],
+                    in_=sums[unit][j][:, h * DH : (h + 1) * DH],
+                    func=ACT.Square,
+                    accum_out=sum_sq[unit][:, j, h : h + 1],
+                )
+
+        def inverse_rms(unit):
+            factors = small.tile([P, PAIR, H], F32)
+            nc.scalar.activation(
+                out=factors[:],
+                in_=sum_sq[unit][:],
+                func=ACT.Abs_reciprocal_sqrt,
+                scale=1.0 / DH,
+                bias=eps[:, 0:1],
+            )
+            inv_rms[unit] = factors
+
+        def normalise(unit):
+            blk, half, pr = place(unit)
+            if pr == 0:
+                res = res_pool.tile([P, H, BLOCK_TILES, DH], F32)
+                results[(blk, half)] = res
+            res = results[(blk, half)]
+            for j in range(PAIR):
+                nc.vector.tensor_tensor(
+                    out=res[:, :, pr * PAIR + j, :],
+                    in0=sums[unit][j][:].rearrange("p (h d) -> p h d", h=H),
+                    in1=inv_rms[unit][:, j, :].unsqueeze(2).to_broadcast([P, H, DH]),
+                    op=ALU.mult,
+                )
+            if pr == PAIRS_IN_BLOCK - 1:
+                grp, part = divmod(blk, BLOCKS_IN_GROUP)
                 run = BLOCK_TILES * DH
                 for h in range(H):
                     nc.sync.dma_start(
@@ -202,3 +212,54 @@ def tile_pieceroutedattention_pa_t_kernel(tc, x, Wq, Wk, out_0, out_1):
                         ],
                         in_=res[:, h, :, :].rearrange("p i d -> p (i d)"),
                     )
+
+        load_weight(0)
+        load_tokens(0)
+        load_weight(1)
+        for blk in range(1, BLOCKS):
+            load_tokens(blk)
+
+        ident = keep.tile([P, P], F32)
+        make_identity(nc, ident[:])
+        eps = keep.tile([P, 1], F32)
+        nc.vector.memset(eps[:], EPS)
+        warm = keep.tile([P, 1], F32)
+        nc.scalar.activation(out=warm[:], in_=eps[:], func=ACT.Abs_reciprocal_sqrt)
+        w_codes = keep.tile([P, PASSES, 2, E], U32, align_bytes=64)
+        w_scales = keep.tile([P, PASSES, 2, E], U8, align_bytes=64)
+
+        for g in range(PASSES):
+            regroup_weight(0, g)
+        for g in range(PASSES):
+            quantise_weight(0, g)
+        for pair in range(PAIRS_AHEAD):
+            turn(pair)
+            for j in range(PAIR):
+                regroup_tokens(pair, j, nc.scalar.copy)
+        quantise_tokens(0)
+        regroup_weight(1, 0)
+        quantise_tokens(1)
+        regroup_weight(1, 1)
+        for g in range(PASSES):
+            quantise_weight(1, g)
+
+        for u in range(UNITS + 1):
+            ahead = u // 2 + PAIRS_AHEAD
+            prepare = u % 2 == 0 and ahead < PAIRS
+            if u < UNITS:
+                project(u)
+            if prepare:
+                turn(ahead)
+            if u < UNITS:
+                sum_squares(u, 0)
+            if u > 0:
+                inverse_rms(u - 1)
+            if prepare:
+                regroup_tokens(ahead, 0, nc.scalar.copy)
+                regroup_tokens(ahead, 1, nc.vector.tensor_copy)
+            if u < UNITS:
+                sum_squares(u, 1)
+            if u > 0:
+                normalise(u - 1)
+            if prepare:
+                quantise_tokens(ahead)

@@ -182,7 +182,7 @@ def tile_pieceroutedattention_pa_t_kernel(tc, x, Wq, Wk, out_0, out_1):
                 in_=sum_sq[unit][:],
                 func=ACT.Abs_reciprocal_sqrt,
                 scale=1.0 / DH,
-                bias=eps[:, 0:1],
+                bias=EPS,
             )
             inv_rms[unit] = factors
 
@@ -199,18 +199,19 @@ def tile_pieceroutedattention_pa_t_kernel(tc, x, Wq, Wk, out_0, out_1):
                     in1=inv_rms[unit][:, j, :].unsqueeze(2).to_broadcast([P, H, DH]),
                     op=ALU.mult,
                 )
-            if pr == PAIRS_IN_BLOCK - 1:
-                grp, part = divmod(blk, BLOCKS_IN_GROUP)
-                run = BLOCK_TILES * DH
+            tiles = PAIR if blk == BLOCKS - 1 else BLOCK_TILES
+            done = (pr + 1) * PAIR
+            if done % tiles == 0:
+                grp, first = divmod(blk * BLOCK_TILES + done - tiles, GROUP_TILES)
                 for h in range(H):
                     nc.sync.dma_start(
                         out=out_runs[half][
                             h,
                             grp * GROUP_BOARDS : (grp + 1) * GROUP_BOARDS,
                             :,
-                            part * run : (part + 1) * run,
+                            first * DH : (first + tiles) * DH,
                         ],
-                        in_=res[:, h, :, :].rearrange("p i d -> p (i d)"),
+                        in_=res[:, h, done - tiles : done, :].rearrange("p i d -> p (i d)"),
                     )
 
         load_weight(0)

from contextlib import ExitStack

import concourse.mybir as mybir
from concourse.masks import make_identity

F32 = mybir.dt.float32
BF16 = mybir.dt.bfloat16
U32 = mybir.dt.uint32
U8 = mybir.dt.uint8
FP8X4 = mybir.dt.float8_e4m3fn_x4
ACT = mybir.ActivationFunctionType
ALU = mybir.AluOpType

P = 128
BOARDS, SQUARES, C = 64, 64, 1024
H, DH = 4, 128
E = H * DH
EPS = 2.0**-23
TOKENS = BOARDS * SQUARES

PACK = 4
K_PASS = P * PACK
PASSES = C // K_PASS
WORD_PLANES = 2

GROUP_TILES = 8
GROUP_TOKENS = P * GROUP_TILES
GROUP_BOARDS = GROUP_TOKENS // SQUARES
RUNS = SQUARES // GROUP_TILES
BLOCK_TILES = 4
PAIR = 2
BLOCKS = TOKENS // (P * BLOCK_TILES)
BLOCKS_IN_GROUP = GROUP_TILES // BLOCK_TILES
PAIRS_IN_BLOCK = BLOCK_TILES // PAIR
PAIRS = BLOCKS * PAIRS_IN_BLOCK
UNITS_IN_BLOCK = 2 * PAIRS_IN_BLOCK
UNITS = BLOCKS * UNITS_IN_BLOCK
PAIRS_AHEAD = 2

FLOPS = 2 * TOKENS * C * 2 * E


def tile_pieceroutedattention_pa_t_kernel(tc, x, Wq, Wk, out_0, out_1):
    nc = tc.nc
    weights = (Wq, Wk)
    x_tiles = x.flatten_outer_dims().rearrange("(g p i) c -> g p i c", p=P, i=GROUP_TILES)
    out_runs = [
        out.rearrange("b h (r i) d -> h b r (i d)", i=GROUP_TILES) for out in (out_0, out_1)
    ]

    with ExitStack() as stack:
        stack.enter_context(tc.manual_schedule())
        keep = stack.enter_context(tc.tile_pool(name="keep", bufs=1))
        w_pool = stack.enter_context(tc.tile_pool(name="w", bufs=2))
        x_pool = stack.enter_context(tc.tile_pool(name="x", bufs=BLOCKS))
        stage = stack.enter_context(tc.tile_pool(name="stage", bufs=2))
        codes_pool = stack.enter_context(tc.tile_pool(name="codes", bufs=2 * PAIRS_IN_BLOCK + 1))
        small = stack.enter_context(tc.tile_pool(name="small", bufs=4))
        res_pool = stack.enter_context(tc.tile_pool(name="res", bufs=6))
        psum_x = stack.enter_context(tc.psum_pool(name="psum_x", bufs=PAIR))
        psum_y = stack.enter_context(tc.psum_pool(name="psum_y", bufs=3 * PAIR))

        w_raw = {}
        w_grouped = {}
        x_blocks = {}
        turned = {}
        grouped = {}
        quantised = {}
        sums = {}
        sum_sq = {}
        inv_rms = {}
        results = {}

        def load_weight(half):
            raw = w_pool.tile([P, PASSES, PACK, E], BF16)
            for g in range(PASSES):
                nc.sync.dma_start(
                    out=raw[:, g, :, :].rearrange("p (u e) n -> p u (e n)", u=WORD_PLANES),
                    in_=weights[half][g * K_PASS : (g + 1) * K_PASS, :].rearrange(
                        "(u p e) n -> p u (e n)", u=WORD_PLANES, p=P
                    ),
                )
            w_raw[half] = raw

        def load_tokens(blk):
            grp, first = divmod(blk * BLOCK_TILES, GROUP_TILES)
            x_sb = x_pool.tile([P, BLOCK_TILES, C], BF16)
            for pr in range(PAIRS_IN_BLOCK):
                nc.sync.dma_start(
                    out=x_sb[:, pr * PAIR : (pr + 1) * PAIR, :],
                    in_=x_tiles[grp, :, first + pr * PAIR : first + (pr + 1) * PAIR, :],
                )
            x_blocks[blk] = x_sb

        def regroup_weight(half, g):
            side_by_side = w_pool.tile([P, E, PACK], BF16, align_bytes=64)
            nc.vector.tensor_copy(
                out=side_by_side[:].rearrange("p (c i) t -> p c t i", i=4),
                in_=w_raw[half][:, g, :, :].rearrange("p t (c i) -> p c t i", i=4),
            )
            w_grouped[(half, g)] = side_by_side

        def quantise_weight(half, g):
            nc.vector.quantize_mx(
                out=w_codes[:, g, half, :].bitcast(FP8X4),
                scales=w_scales[:, g, half, :],
                in_=w_grouped[(half, g)][:].rearrange("p n t -> p (n t)"),
            )

        def turn(pair):
            blk, pr = divmod(pair, PAIRS_IN_BLOCK)
            banks = []
            for j in range(PAIR):
                words = x_blocks[blk][:, pr * PAIR + j, :].bitcast(F32)
                bank = psum_x.tile([P, PASSES * WORD_PLANES, P], F32)
                for c in range(PASSES * WORD_PLANES):
                    nc.tensor.transpose(bank[:, c, :], words[:, c * P : (c + 1) * P], ident[:])
                banks.append(bank)
            turned[pair] = banks
            side_by_side = stage.tile([P, PAIR, PASSES, P, PACK], BF16, align_bytes=64)
            grouped[pair] = side_by_side

        def regroup_tokens(pair, j, copy):
            copy(
                out=grouped[pair][:, j]
                .rearrange("p g r t -> p (g r t)")
                .bitcast(F32)
                .rearrange("p (g r u) -> p g r u", g=PASSES, u=WORD_PLANES),
                in_=turned[pair][j][:].rearrange("p (g u) r -> p g r u", u=WORD_PLANES),
            )

        def quantise_tokens(pair):
            x_codes = codes_pool.tile([P, PAIR, PASSES, P], U32, align_bytes=64)
            x_scales = codes_pool.tile([P, PAIR, PASSES, P], U8, align_bytes=64)
            nc.vector.quantize_mx(
                out=x_codes[:].rearrange("p j g r -> p (j g r)").bitcast(FP8X4),
                scales=x_scales[:].rearrange("p j g r -> p (j g r)"),
                in_=grouped[pair][:].rearrange("p j g r t -> p (j g r t)"),
            )
            quantised[pair] = (x_codes, x_scales)

        def place(unit):
            blk, rest = divmod(unit, UNITS_IN_BLOCK)
            half, pr = divmod(rest, PAIRS_IN_BLOCK)
            return blk, half, pr

        def project(unit):
            blk, half, pr = place(unit)
            x_codes, x_scales = quantised[blk * PAIRS_IN_BLOCK + pr]
            banks = []
            for j in range(PAIR):
                y = psum_y.tile([P, E], F32)
                for g in range(PASSES):
                    nc.tensor.matmul_mx(
                        out=y[:],
                        lhsT=x_codes[:, j, g, :].bitcast(FP8X4),
                        lhsT_scale=x_scales[:, j, g, :],
                        rhs=w_codes[:, g, half, :].bitcast(FP8X4),
                        rhs_scale=w_scales[:, g, half, :],
                        start=(g == 0),
                        stop=(g == PASSES - 1),
                    )
                banks.append(y)
            sums[unit] = banks
            totals = small.tile([P, PAIR, H], F32)
            sum_sq[unit] = totals

        def sum_squares(unit, j):
            squares = small.tile([P, H, DH], BF16)
            for h in range(H):
                nc.scalar.activation(
                    out=squares[:, h, :],
                    in_=sums[unit][j][:, h * DH : (h + 1) * DH],
                    func=ACT.Square,
                    accum_out=sum_sq[unit][:, j, h : h + 1],
                )

        def inverse_rms(unit):
            factors = small.tile([P, PAIR, H], F32)
            nc.scalar.activation(
                out=factors[:],
                in_=sum_sq[unit][:],
                func=ACT.Abs_reciprocal_sqrt,
                scale=1.0 / DH,
                bias=EPS,
            )
            inv_rms[unit] = factors

        def normalise(unit):
            blk, half, pr = place(unit)
            if pr == 0:
                res = res_pool.tile([P, H, BLOCK_TILES, DH], F32)
                results[(blk, half)] = res
            res = results[(blk, half)]
            for j in range(PAIR):
                nc.vector.tensor_tensor(
                    out=res[:, :, pr * PAIR + j, :],
                    in0=sums[unit][j][:].rearrange("p (h d) -> p h d", h=H),
                    in1=inv_rms[unit][:, j, :].unsqueeze(2).to_broadcast([P, H, DH]),
                    op=ALU.mult,
                )
            tiles = PAIR if blk == BLOCKS - 1 else BLOCK_TILES
            done = (pr + 1) * PAIR
            if done % tiles == 0:
                grp, first = divmod(blk * BLOCK_TILES + done - tiles, GROUP_TILES)
                for h in range(H):
                    nc.sync.dma_start(
                        out=out_runs[half][
                            h,
                            grp * GROUP_BOARDS : (grp + 1) * GROUP_BOARDS,
                            :,
                            first * DH : (first + tiles) * DH,
                        ],
                        in_=res[:, h, done - tiles : done, :].rearrange("p i d -> p (i d)"),
                    )

        load_weight(0)
        load_tokens(0)
        load_weight(1)
        for blk in range(1, BLOCKS):
            load_tokens(blk)

        ident = keep.tile([P, P], F32)
        make_identity(nc, ident[:])
        eps = keep.tile([P, 1], F32)
        nc.vector.memset(eps[:], EPS)
        warm = keep.tile([P, 1], F32)
        nc.scalar.activation(out=warm[:], in_=eps[:], func=ACT.Abs_reciprocal_sqrt)
        w_codes = keep.tile([P, PASSES, 2, E], U32, align_bytes=64)
        w_scales = keep.tile([P, PASSES, 2, E], U8, align_bytes=64)

        for g in range(PASSES):
            regroup_weight(0, g)
        for g in range(PASSES):
            quantise_weight(0, g)
        for pair in range(PAIRS_AHEAD):
            turn(pair)
            for j in range(PAIR):
                regroup_tokens(pair, j, nc.scalar.copy)
        quantise_tokens(0)
        regroup_weight(1, 0)
        quantise_tokens(1)
        regroup_weight(1, 1)
        for g in range(PASSES):
            quantise_weight(1, g)

        for u in range(UNITS + 1):
            ahead = u // 2 + PAIRS_AHEAD
            prepare = u % 2 == 0 and ahead < PAIRS
            if u < UNITS:
                project(u)
            if prepare:
                turn(ahead)
            if u < UNITS:
                sum_squares(u, 0)
            if u > 0:
                inverse_rms(u - 1)
            if prepare:
                regroup_tokens(ahead, 0, nc.scalar.copy)
                regroup_tokens(ahead, 1, nc.vector.tensor_copy)
            if u < UNITS:
                sum_squares(u, 1)
            if u > 0:
                normalise(u - 1)
            if prepare:
                quantise_tokens(ahead)
